import numpy as np
import ml_dtypes


def mxq(x, axis, fmt="e4m3"):
    dtype, down = {"e4m3": (ml_dtypes.float8_e4m3fn, 7), "e5m2": (ml_dtypes.float8_e5m2, 14)}[fmt]
    v = np.moveaxis(np.asarray(x, np.float32).astype(ml_dtypes.bfloat16).astype(np.float64), axis, -1)
    blocks = v.reshape(v.shape[:-1] + (-1, 32))
    amax = np.abs(blocks).max(-1, keepdims=True)
    byte = np.maximum(np.where(amax > 0, np.frexp(amax)[1] - 1 + 127, 0) - down, 1)
    scale = np.exp2(byte - 127.0)
    codes = (blocks / scale).astype(np.float32).astype(dtype).astype(np.float64)
    return np.moveaxis((codes * scale).reshape(v.shape), -1, axis)


WIDE = False


def mx_kscale(k):
    if not WIDE:
        return np.ones(k)
    levels = np.array([10, -10, 5, -5, 0])
    a = np.random.permutation(np.resize(levels, k // 512 * 4)).reshape(k // 512, 4)
    idx = np.arange(k)
    return np.exp2(a[idx // 512, idx % 128 // 32])


BF16 = ml_dtypes.bfloat16


def bf(x):
    return np.asarray(x, np.float32).astype(BF16)


def f64(x):
    return np.asarray(x).astype(np.float64)


B, LC, LL, LLAMA_DIM, DIM, HEADS, FF = 16, 77, 256, 512, 512, 16, 6144
EPS = 1e-5


def layernorm(x, g, b):
    m = x.mean(-1, keepdims=True)
    v = ((x - m) ** 2).mean(-1, keepdims=True)
    return (x - m) / np.sqrt(v + EPS) * g + b


def setup_inputs():
    s, t = mx_kscale(LLAMA_DIM), mx_kscale(DIM)
    return {
        "llm_embed": bf(np.random.standard_normal((B, LL, LLAMA_DIM)) * s),
        "llm_proj_w": bf(np.random.standard_normal((DIM, LLAMA_DIM)) / np.sqrt(LLAMA_DIM) / s),
        "llm_proj_b": bf(0.1 * np.random.standard_normal(DIM)),
        "kvn_g": bf((1.0 + 0.1 * np.random.standard_normal(DIM)) * t),
        "kvn_b": bf(0.1 * np.random.standard_normal(DIM) * t),
        "q_w": bf(np.random.standard_normal((DIM, DIM)) / np.sqrt(DIM) / t),
        "q_b": bf(0.1 * np.random.standard_normal(DIM)),
    }


def reference(llm_embed, llm_proj_w, llm_proj_b, kvn_g, kvn_b, q_w, q_b):
    llm = (mxq(f64(llm_embed), 2, "e4m3") @ mxq(f64(llm_proj_w), 1, "e4m3").T) + f64(llm_proj_b)
    llm_n = layernorm(llm, f64(kvn_g), f64(kvn_b))
    q = (mxq(llm_n, 2, "e4m3") @ mxq(f64(q_w), 1, "e4m3").T) + f64(q_b)
    return llm, q

@@ -1,0 +1,275 @@
+from contextlib import ExitStack
+
+import concourse.mybir as mybir
+from concourse.masks import make_identity
+
+F32 = mybir.dt.float32
+BF16 = mybir.dt.bfloat16
+U32 = mybir.dt.uint32
+U8 = mybir.dt.uint8
+FP8X4 = mybir.dt.float8_e4m3fn_x4
+ACT = mybir.ActivationFunctionType
+ALU = mybir.AluOpType
+
+P = 128
+PACK = 4
+D = P * PACK
+TOKENS = 16 * 256
+TILES = 4
+GROUP = P * TILES
+GROUPS = TOKENS // GROUP
+HALF = GROUP // 2
+EPS = 1e-5
+W2_TRANSPOSE_STEP = 1
+W2_QUANTISE_STEP = 2
+
+FLOPS = 2 * 2 * TOKENS * D * D
+
+
+def tile_crossfusion_pa_t_kernel(tc, x, w1, b1, gamma, beta, w2, b2, llm_out, q_out):
+    nc = tc.nc
+    x_groups = x.flatten_outer_dims().rearrange("(g p j) k -> g p j k", p=P, j=TILES)
+    llm_groups = llm_out.flatten_outer_dims().rearrange("(g p j) f -> g p j f", p=P, j=TILES)
+    q_groups = q_out.flatten_outer_dims().rearrange("(g p j) f -> g p j f", p=P, j=TILES)
+
+    with ExitStack() as stack:
+        stack.enter_context(tc.manual_schedule())
+        const = stack.enter_context(tc.tile_pool(name="const", bufs=1))
+        x_pool = stack.enter_context(tc.tile_pool(name="x_pool", bufs=GROUPS))
+        work = stack.enter_context(tc.tile_pool(name="work", bufs=2))
+        wide = stack.enter_context(tc.tile_pool(name="wide", bufs=3))
+        small = stack.enter_context(tc.tile_pool(name="small", bufs=4))
+        psum_t = stack.enter_context(tc.psum_pool(name="psum_t", bufs=2))
+        psum_acc = stack.enter_context(tc.psum_pool(name="psum_acc", bufs=4))
+        psum_z = stack.enter_context(tc.psum_pool(name="psum_z", bufs=2))
+
+        x_sb = []
+        for g in range(GROUPS):
+            x_sb.append(x_pool.tile([P, TILES, D], BF16, name="x_sb", tag="x_sb"))
+        w1_sb = const.tile([P, PACK, D], BF16)
+        w2_sb = const.tile([P, PACK, D], BF16)
+        bias_rows = const.tile([P, 2, D], BF16)
+        param_rows = const.tile([P, P], BF16)
+        nc.vector.memset(bias_rows[:], 0.0)
+        nc.vector.memset(param_rows[:], 0.0)
+        nc.sync.dma_start(out=w1_sb[:], in_=w1.rearrange("(ob p) k -> p ob k", p=P))
+        nc.sync.dma_start(out=x_sb[0][:], in_=x_groups[0])
+        nc.sync.dma_start(out=bias_rows[0:1, 0, :], in_=b1.rearrange("(o f) -> o f", o=1))
+        nc.sync.dma_start(out=x_sb[1][:], in_=x_groups[1])
+        nc.sync.dma_start(out=w2_sb[:], in_=w2.rearrange("(ob p) k -> p ob k", p=P))
+        nc.sync.dma_start(out=bias_rows[0:1, 1, :], in_=b2.rearrange("(o f) -> o f", o=1))
+        nc.sync.dma_start(out=param_rows[0:PACK, :], in_=gamma.rearrange("(t p) -> t p", p=P))
+        nc.sync.dma_start(out=param_rows[PACK : 2 * PACK, :], in_=beta.rearrange("(t p) -> t p", p=P))
+        for g in range(2, GROUPS):
+            nc.sync.dma_start(out=x_sb[g][:], in_=x_groups[g])
+
+        ident_f32 = const.tile([P, P], F32)
+        make_identity(nc, ident_f32[:])
+        ident_bf = const.tile([P, P], BF16)
+        make_identity(nc, ident_bf[:])
+        ones = const.tile([P, P], BF16)
+        nc.vector.memset(ones[:], 1.0)
+        warm = const.tile([P, 1], F32)
+        nc.vector.memset(warm[:], 1.0)
+        nc.scalar.sqrt(out=warm[:], in_=warm[:])
+
+        def word_transposes(rows, grouped, on_vector):
+            words = rows.bitcast(F32)
+            grouped_words = grouped.bitcast(F32)
+            for h in range(2):
+                planes_ps = psum_t.tile([P, 2, HALF], F32, name="planes_ps", tag="tp")
+                for b in range(2):
+                    for u in range(2):
+                        nc.tensor.transpose(
+                            planes_ps[:, u, b * P : (b + 1) * P],
+                            words[:, 2 * h + b, u * P : (u + 1) * P],
+                            ident_f32[:],
+                        )
+                if on_vector:
+                    nc.vector.tensor_copy(
+                        out=grouped_words[:, h * HALF : (h + 1) * HALF, :],
+                        in_=planes_ps[:].rearrange("p u c -> p c u"),
+                    )
+                else:
+                    nc.scalar.copy(
+                        out=grouped_words[:, h * HALF : (h + 1) * HALF, :],
+                        in_=planes_ps[:].rearrange("p u c -> p c u"),
+                    )
+
+        def quantise(grouped, codes, scales):
+            nc.vector.quantize_mx(
+                out=codes.bitcast(FP8X4),
+                scales=scales,
+                in_=grouped.rearrange("p c t -> p (c t)"),
+            )
+
+        w1_grouped = const.tile([P, D, PACK], BF16, align_bytes=64)
+        w1_codes = const.tile([P, D], U32, align_bytes=64)
+        w1_scales = const.tile([P, D], U8, align_bytes=64)
+        word_transposes(w1_sb[:], w1_grouped[:], True)
+        quantise(w1_grouped[:], w1_codes[:], w1_scales[:])
+
+        bias_bc = const.tile([P, 2, D], F32)
+        params = const.tile([P, 2 * PACK], F32)
+        w2_grouped = const.tile([P, D, PACK], BF16, align_bytes=64)
+        w2_codes = const.tile([P, D], U32, align_bytes=64)
+        w2_scales = const.tile([P, D], U8, align_bytes=64)
+
+        def spread_bias(i):
+            bias_ps = psum_acc.tile([P, D], F32, name="bias_ps", tag="acc")
+            nc.tensor.matmul(bias_ps[:], lhsT=ones[:], rhs=bias_rows[:, i, :], start=True, stop=True)
+            nc.vector.tensor_copy(out=bias_bc[:, i, :], in_=bias_ps[:])
+
+        def w2_to_partitions():
+            param_ps = psum_t.tile([P, P], BF16, name="param_ps", tag="tp")
+            nc.tensor.transpose(param_ps[:], param_rows[:], ident_bf[:])
+            nc.scalar.copy(out=params[:], in_=param_ps[:, 0 : 2 * PACK])
+            for h in range(2):
+                w2_ps = psum_t.tile([P, PACK, HALF], BF16, name="w2_ps", tag="tp")
+                for b in range(2):
+                    for t in range(PACK):
+                        nc.tensor.transpose(
+                            w2_ps[:, t, b * P : (b + 1) * P],
+                            w2_sb[:, 2 * h + b, t * P : (t + 1) * P],
+                            ident_bf[:],
+                        )
+                nc.scalar.copy(
+                    out=w2_grouped[:, h * HALF : (h + 1) * HALF, :],
+                    in_=w2_ps[:].rearrange("p t c -> p c t"),
+                )
+
+        x_grouped, x_codes, x_scales = {}, {}, {}
+        llm, sums, neg_mean, std, z = {}, {}, {}, {}, {}
+        planes, n_codes, n_scales = {}, {}, {}
+
+        def x_to_partitions(g):
+            x_grouped[g] = wide.tile([P, GROUP, PACK], BF16, name="x_grouped", align_bytes=64)
+            word_transposes(x_sb[g][:], x_grouped[g][:], False)
+
+        def quantise_x(g):
+            x_codes[g] = work.tile([P, GROUP], U32, name="x_codes", align_bytes=64)
+            x_scales[g] = work.tile([P, GROUP], U8, name="x_scales", align_bytes=64)
+            quantise(x_grouped[g][:], x_codes[g][:], x_scales[g][:])
+
+        def first_matmul(g):
+            llm[g] = wide.tile([P, TILES, D], F32, name="llm", bufs=4)
+            sums[g] = small.tile([P, TILES], F32, name="sums")
+            for j in range(TILES):
+                cols = slice(j * P, (j + 1) * P)
+                acc = psum_acc.tile([P, D], F32, name="acc", tag="acc")
+                nc.tensor.matmul_mx(
+                    out=acc[:],
+                    lhsT=x_codes[g][:, cols].bitcast(FP8X4),
+                    lhsT_scale=x_scales[g][:, cols],
+                    rhs=w1_codes[:].bitcast(FP8X4),
+                    rhs_scale=w1_scales[:],
+                    start=True,
+                    stop=True,
+                )
+                nc.vector.scalar_tensor_tensor(
+                    out=llm[g][:, j, :],
+                    in0=acc[:],
+                    scalar=1.0,
+                    in1=bias_bc[:, 0, :],
+                    op0=ALU.mult,
+                    op1=ALU.add,
+                    accum_out=sums[g][:, j : j + 1],
+                )
+            nc.sync.dma_start(out=llm_groups[g], in_=llm[g][:])
+
+        def statistics(g):
+            neg_mean[g] = small.tile([P, TILES], F32, name="neg_mean")
+            nc.scalar.mul(out=neg_mean[g][:], in_=sums[g][:], mul=-1.0 / D)
+            squares = work.tile([P, TILES, D], BF16)
+            sum_sq = small.tile([P, TILES], F32)
+            for j in range(TILES):
+                nc.scalar.activation(
+                    out=squares[:, j, :],
+                    in_=llm[g][:, j, :],
+                    func=ACT.Square,
+                    bias=neg_mean[g][:, j : j + 1],
+                    scale=1.0,
+                    accum_out=sum_sq[:, j : j + 1],
+                )
+            std[g] = small.tile([P, TILES], F32, name="std")
+            nc.scalar.activation(out=std[g][:], in_=sum_sq[:], func=ACT.Sqrt, bias=EPS, scale=1.0 / D)
+
+        def normalise(g):
+            rstd = small.tile([P, TILES], F32)
+            nc.vector.reciprocal(out=rstd[:], in_=std[g][:])
+            z[g] = work.tile([P, TILES, D], F32, name="z")
+            for j in range(TILES):
+                nc.gpsimd.tensor_scalar(
+                    out=z[g][:, j, :],
+                    in0=llm[g][:, j, :],
+                    scalar1=neg_mean[g][:, j : j + 1],
+                    scalar2=rstd[:, j : j + 1],
+                    op0=ALU.add,
+                    op1=ALU.mult,
+                )
+
+        def features_to_partitions(g):
+            planes[g] = work.tile([P, PACK, GROUP], BF16, name="planes")
+            for t in range(PACK):
+                z_ps = psum_z.tile([P, GROUP], F32, name="z_ps", tag="z_ps")
+                for j in range(TILES):
+                    nc.tensor.transpose(
+                        z_ps[:, j * P : (j + 1) * P], z[g][:, j, t * P : (t + 1) * P], ident_f32[:]
+                    )
+                nc.scalar.activation(
+                    out=planes[g][:, t, :],
+                    in_=z_ps[:],
+                    func=ACT.Identity,
+                    bias=params[:, PACK + t : PACK + t + 1],
+                    scale=params[:, t : t + 1],
+                )
+
+        def quantise_n(g):
+            n_grouped = work.tile([P, GROUP, PACK], BF16, align_bytes=64)
+            nc.vector.tensor_copy(
+                out=n_grouped[:].rearrange("p (c i) t -> p c t i", i=4),
+                in_=planes[g][:].rearrange("p t (c i) -> p c t i", i=4),
+            )
+            n_codes[g] = work.tile([P, GROUP], U32, name="n_codes", align_bytes=64)
+            n_scales[g] = work.tile([P, GROUP], U8, name="n_scales", align_bytes=64)
+            quantise(n_grouped[:], n_codes[g][:], n_scales[g][:])
+
+        def second_matmul(g):
+            q = wide.tile([P, TILES, D], F32)
+            for j in range(TILES):
+                cols = slice(j * P, (j + 1) * P)
+                acc = psum_acc.tile([P, D], F32, name="acc", tag="acc")
+                nc.tensor.matmul_mx(
+                    out=acc[:],
+                    lhsT=n_codes[g][:, cols].bitcast(FP8X4),
+                    lhsT_scale=n_scales[g][:, cols],
+                    rhs=w2_codes[:].bitcast(FP8X4),
+                    rhs_scale=w2_scales[:],
+                    start=True,
+                    stop=True,
+                )
+                nc.vector.tensor_add(out=q[:, j, :], in0=acc[:], in1=bias_bc[:, 1, :])
+                nc.sync.dma_start(out=q_groups[g][:, j, :], in_=q[:, j, :])
+
+        stages = (
+            x_to_partitions,
+            quantise_x,
+            first_matmul,
+            statistics,
+            normalise,
+            features_to_partitions,
+            quantise_n,
+            second_matmul,
+        )
+        for step in range(GROUPS + len(stages) - 1):
+            for lag, stage in enumerate(stages):
+                g = step - lag
+                if 0 <= g < GROUPS:
+                    stage(g)
+            if step == 0:
+                spread_bias(0)
+            if step == W2_TRANSPOSE_STEP:
+                w2_to_partitions()
+            if step == W2_QUANTISE_STEP:
+                quantise(w2_grouped[:], w2_codes[:], w2_scales[:])
+                spread_bias(1)

@@ -15,13 +15,13 @@ P = 128
 PACK = 4
 D = P * PACK
 TOKENS = 16 * 256
-TILES = 4
+TILES = 2
 GROUP = P * TILES
 GROUPS = TOKENS // GROUP
-HALF = GROUP // 2
 EPS = 1e-5
-W2_TRANSPOSE_STEP = 1
-W2_QUANTISE_STEP = 2
+LAST_LAG = 7
+W2_TRANSPOSE_STEP = 3
+W2_QUANTISE_STEP = 4
 
 FLOPS = 2 * 2 * TOKENS * D * D
 
@@ -36,8 +36,8 @@ def tile_crossfusion_pa_t_kernel(tc, x, w1, b1, gamma, beta, w2, b2, llm_out, q_
         stack.enter_context(tc.manual_schedule())
         const = stack.enter_context(tc.tile_pool(name="const", bufs=1))
         x_pool = stack.enter_context(tc.tile_pool(name="x_pool", bufs=GROUPS))
-        work = stack.enter_context(tc.tile_pool(name="work", bufs=2))
-        wide = stack.enter_context(tc.tile_pool(name="wide", bufs=3))
+        work = stack.enter_context(tc.tile_pool(name="work", bufs=3))
+        wide = stack.enter_context(tc.tile_pool(name="wide", bufs=5))
         small = stack.enter_context(tc.tile_pool(name="small", bufs=4))
         psum_t = stack.enter_context(tc.psum_pool(name="psum_t", bufs=2))
         psum_acc = stack.enter_context(tc.psum_pool(name="psum_acc", bufs=4))
@@ -56,11 +56,12 @@ def tile_crossfusion_pa_t_kernel(tc, x, w1, b1, gamma, beta, w2, b2, llm_out, q_
         nc.sync.dma_start(out=x_sb[0][:], in_=x_groups[0])
         nc.sync.dma_start(out=bias_rows[0:1, 0, :], in_=b1.rearrange("(o f) -> o f", o=1))
         nc.sync.dma_start(out=x_sb[1][:], in_=x_groups[1])
+        nc.sync.dma_start(out=x_sb[2][:], in_=x_groups[2])
         nc.sync.dma_start(out=w2_sb[:], in_=w2.rearrange("(ob p) k -> p ob k", p=P))
         nc.sync.dma_start(out=bias_rows[0:1, 1, :], in_=b2.rearrange("(o f) -> o f", o=1))
         nc.sync.dma_start(out=param_rows[0:PACK, :], in_=gamma.rearrange("(t p) -> t p", p=P))
         nc.sync.dma_start(out=param_rows[PACK : 2 * PACK, :], in_=beta.rearrange("(t p) -> t p", p=P))
-        for g in range(2, GROUPS):
+        for g in range(3, GROUPS):
             nc.sync.dma_start(out=x_sb[g][:], in_=x_groups[g])
 
         ident_f32 = const.tile([P, P], F32)
@@ -75,26 +76,16 @@ def tile_crossfusion_pa_t_kernel(tc, x, w1, b1, gamma, beta, w2, b2, llm_out, q_
 
         def word_transposes(rows, grouped, on_vector):
             words = rows.bitcast(F32)
-            grouped_words = grouped.bitcast(F32)
-            for h in range(2):
-                planes_ps = psum_t.tile([P, 2, HALF], F32, name="planes_ps", tag="tp")
-                for b in range(2):
-                    for u in range(2):
-                        nc.tensor.transpose(
-                            planes_ps[:, u, b * P : (b + 1) * P],
-                            words[:, 2 * h + b, u * P : (u + 1) * P],
-                            ident_f32[:],
-                        )
-                if on_vector:
-                    nc.vector.tensor_copy(
-                        out=grouped_words[:, h * HALF : (h + 1) * HALF, :],
-                        in_=planes_ps[:].rearrange("p u c -> p c u"),
+            planes_ps = psum_t.tile([P, 2, 2 * P], F32, name="planes_ps", tag="tp")
+            for b in range(2):
+                for u in range(2):
+                    nc.tensor.transpose(
+                        planes_ps[:, u, b * P : (b + 1) * P], words[:, b, u * P : (u + 1) * P], ident_f32[:]
                     )
-                else:
-                    nc.scalar.copy(
-                        out=grouped_words[:, h * HALF : (h + 1) * HALF, :],
-                        in_=planes_ps[:].rearrange("p u c -> p c u"),
-                    )
+            if on_vector:
+                nc.vector.tensor_copy(out=grouped.bitcast(F32), in_=planes_ps[:].rearrange("p u c -> p c u"))
+            else:
+                nc.scalar.copy(out=grouped.bitcast(F32), in_=planes_ps[:].rearrange("p u c -> p c u"))
 
         def quantise(grouped, codes, scales):
             nc.vector.quantize_mx(
@@ -106,7 +97,8 @@ def tile_crossfusion_pa_t_kernel(tc, x, w1, b1, gamma, beta, w2, b2, llm_out, q_
         w1_grouped = const.tile([P, D, PACK], BF16, align_bytes=64)
         w1_codes = const.tile([P, D], U32, align_bytes=64)
         w1_scales = const.tile([P, D], U8, align_bytes=64)
-        word_transposes(w1_sb[:], w1_grouped[:], True)
+        word_transposes(w1_sb[:, 0:2, :], w1_grouped[:, 0 : 2 * P, :], True)
+        word_transposes(w1_sb[:, 2:4, :], w1_grouped[:, 2 * P : 4 * P, :], False)
         quantise(w1_grouped[:], w1_codes[:], w1_scales[:])
 
         bias_bc = const.tile([P, 2, D], F32)
@@ -125,7 +117,7 @@ def tile_crossfusion_pa_t_kernel(tc, x, w1, b1, gamma, beta, w2, b2, llm_out, q_
             nc.tensor.transpose(param_ps[:], param_rows[:], ident_bf[:])
             nc.scalar.copy(out=params[:], in_=param_ps[:, 0 : 2 * PACK])
             for h in range(2):
-                w2_ps = psum_t.tile([P, PACK, HALF], BF16, name="w2_ps", tag="tp")
+                w2_ps = psum_t.tile([P, PACK, 2 * P], BF16, name="w2_ps", tag="tp")
                 for b in range(2):
                     for t in range(PACK):
                         nc.tensor.transpose(
@@ -134,16 +126,16 @@ def tile_crossfusion_pa_t_kernel(tc, x, w1, b1, gamma, beta, w2, b2, llm_out, q_
                             ident_bf[:],
                         )
                 nc.scalar.copy(
-                    out=w2_grouped[:, h * HALF : (h + 1) * HALF, :],
+                    out=w2_grouped[:, 2 * h * P : 2 * (h + 1) * P, :],
                     in_=w2_ps[:].rearrange("p t c -> p c t"),
                 )
 
         x_grouped, x_codes, x_scales = {}, {}, {}
         llm, sums, neg_mean, std, z = {}, {}, {}, {}, {}
-        planes, n_codes, n_scales = {}, {}, {}
+        planes, n_grouped, n_codes, n_scales = {}, {}, {}, {}
 
         def x_to_partitions(g):
-            x_grouped[g] = wide.tile([P, GROUP, PACK], BF16, name="x_grouped", align_bytes=64)
+            x_grouped[g] = work.tile([P, GROUP, PACK], BF16, name="x_grouped", align_bytes=64)
             word_transposes(x_sb[g][:], x_grouped[g][:], False)
 
         def quantise_x(g):
@@ -152,7 +144,7 @@ def tile_crossfusion_pa_t_kernel(tc, x, w1, b1, gamma, beta, w2, b2, llm_out, q_
             quantise(x_grouped[g][:], x_codes[g][:], x_scales[g][:])
 
         def first_matmul(g):
-            llm[g] = wide.tile([P, TILES, D], F32, name="llm", bufs=4)
+            llm[g] = wide.tile([P, TILES, D], F32, name="llm")
             sums[g] = small.tile([P, TILES], F32, name="sums")
             for j in range(TILES):
                 cols = slice(j * P, (j + 1) * P)
@@ -210,29 +202,35 @@ def tile_crossfusion_pa_t_kernel(tc, x, w1, b1, gamma, beta, w2, b2, llm_out, q_
 
         def features_to_partitions(g):
             planes[g] = work.tile([P, PACK, GROUP], BF16, name="planes")
-            for t in range(PACK):
-                z_ps = psum_z.tile([P, GROUP], F32, name="z_ps", tag="z_ps")
-                for j in range(TILES):
-                    nc.tensor.transpose(
-                        z_ps[:, j * P : (j + 1) * P], z[g][:, j, t * P : (t + 1) * P], ident_f32[:]
+            for h in range(2):
+                z_ps = psum_z.tile([P, 2, GROUP], F32, name="z_ps", tag="z_ps")
+                for i in range(2):
+                    t = 2 * h + i
+                    for j in range(TILES):
+                        nc.tensor.transpose(
+                            z_ps[:, i, j * P : (j + 1) * P], z[g][:, j, t * P : (t + 1) * P], ident_f32[:]
+                        )
+                for i in range(2):
+                    t = 2 * h + i
+                    nc.scalar.activation(
+                        out=planes[g][:, t, :],
+                        in_=z_ps[:, i, :],
+                        func=ACT.Identity,
+                        bias=params[:, PACK + t : PACK + t + 1],
+                        scale=params[:, t : t + 1],
                     )
-                nc.scalar.activation(
-                    out=planes[g][:, t, :],
-                    in_=z_ps[:],
-                    func=ACT.Identity,
-                    bias=params[:, PACK + t : PACK + t + 1],
-                    scale=params[:, t : t + 1],
-                )
 
-        def quantise_n(g):
-            n_grouped = work.tile([P, GROUP, PACK], BF16, align_bytes=64)
+        def regroup_n(g):
+            n_grouped[g] = work.tile([P, GROUP, PACK], BF16, name="n_grouped", align_bytes=64)
             nc.vector.tensor_copy(
-                out=n_grouped[:].rearrange("p (c i) t -> p c t i", i=4),
+                out=n_grouped[g][:].rearrange("p (c i) t -> p c t i", i=4),
                 in_=planes[g][:].rearrange("p t (c i) -> p c t i", i=4),
             )
+
+        def quantise_n(g):
             n_codes[g] = work.tile([P, GROUP], U32, name="n_codes", align_bytes=64)
             n_scales[g] = work.tile([P, GROUP], U8, name="n_scales", align_bytes=64)
-            quantise(n_grouped[:], n_codes[g][:], n_scales[g][:])
+            quantise(n_grouped[g][:], n_codes[g][:], n_scales[g][:])
 
         def second_matmul(g):
             q = wide.tile([P, TILES, D], F32)
@@ -251,21 +249,20 @@ def tile_crossfusion_pa_t_kernel(tc, x, w1, b1, gamma, beta, w2, b2, llm_out, q_
                 nc.vector.tensor_add(out=q[:, j, :], in0=acc[:], in1=bias_bc[:, 1, :])
                 nc.sync.dma_start(out=q_groups[g][:, j, :], in_=q[:, j, :])
 
-        stages = (
-            x_to_partitions,
-            quantise_x,
-            first_matmul,
-            statistics,
-            normalise,
-            features_to_partitions,
-            quantise_n,
-            second_matmul,
-        )
-        for step in range(GROUPS + len(stages) - 1):
-            for lag, stage in enumerate(stages):
-                g = step - lag
-                if 0 <= g < GROUPS:
-                    stage(g)
+        def run(stage, g):
+            if 0 <= g < GROUPS:
+                stage(g)
+
+        for step in range(GROUPS + LAST_LAG):
+            run(x_to_partitions, step)
+            run(regroup_n, step - 6)
+            run(quantise_x, step - 1)
+            run(quantise_n, step - 6)
+            run(normalise, step - 4)
+            run(first_matmul, step - 2)
+            run(second_matmul, step - 7)
+            run(statistics, step - 3)
+            run(features_to_partitions, step - 5)
             if step == 0:
                 spread_bias(0)
             if step == W2_TRANSPOSE_STEP:

@@ -260,9 +260,9 @@ def tile_crossfusion_pa_t_kernel(tc, x, w1, b1, gamma, beta, w2, b2, llm_out, q_
             run(quantise_n, step - 6)
             run(normalise, step - 4)
             run(first_matmul, step - 2)
-            run(second_matmul, step - 7)
             run(statistics, step - 3)
             run(features_to_partitions, step - 5)
+            run(second_matmul, step - 7)
             if step == 0:
                 spread_bias(0)
             if step == W2_TRANSPOSE_STEP:

@@ -33,7 +33,6 @@ def tile_crossfusion_pa_t_kernel(tc, x, w1, b1, gamma, beta, w2, b2, llm_out, q_
     q_groups = q_out.flatten_outer_dims().rearrange("(g p j) f -> g p j f", p=P, j=TILES)
 
     with ExitStack() as stack:
-        stack.enter_context(tc.manual_schedule())
         const = stack.enter_context(tc.tile_pool(name="const", bufs=1))
         x_pool = stack.enter_context(tc.tile_pool(name="x_pool", bufs=GROUPS))
         work = stack.enter_context(tc.tile_pool(name="work", bufs=3))
@@ -260,9 +259,9 @@ def tile_crossfusion_pa_t_kernel(tc, x, w1, b1, gamma, beta, w2, b2, llm_out, q_
             run(quantise_n, step - 6)
             run(normalise, step - 4)
             run(first_matmul, step - 2)
+            run(second_matmul, step - 7)
             run(statistics, step - 3)
             run(features_to_partitions, step - 5)
-            run(second_matmul, step - 7)
             if step == 0:
                 spread_bias(0)
             if step == W2_TRANSPOSE_STEP:

from contextlib import ExitStack

import concourse.mybir as mybir
from concourse.masks import make_identity

F32 = mybir.dt.float32
BF16 = mybir.dt.bfloat16
U32 = mybir.dt.uint32
U8 = mybir.dt.uint8
FP8X4 = mybir.dt.float8_e4m3fn_x4
ACT = mybir.ActivationFunctionType
ALU = mybir.AluOpType

P = 128
PACK = 4
D = P * PACK
TOKENS = 16 * 256
TILES = 2
GROUP = P * TILES
GROUPS = TOKENS // GROUP
EPS = 1e-5
LAST_LAG = 7
W2_TRANSPOSE_STEP = 3
W2_QUANTISE_STEP = 4

FLOPS = 2 * 2 * TOKENS * D * D


def tile_crossfusion_pa_t_kernel(tc, x, w1, b1, gamma, beta, w2, b2, llm_out, q_out):
    nc = tc.nc
    x_groups = x.flatten_outer_dims().rearrange("(g p j) k -> g p j k", p=P, j=TILES)
    llm_groups = llm_out.flatten_outer_dims().rearrange("(g p j) f -> g p j f", p=P, j=TILES)
    q_groups = q_out.flatten_outer_dims().rearrange("(g p j) f -> g p j f", p=P, j=TILES)

    with ExitStack() as stack:
        const = stack.enter_context(tc.tile_pool(name="const", bufs=1))
        x_pool = stack.enter_context(tc.tile_pool(name="x_pool", bufs=GROUPS))
        work = stack.enter_context(tc.tile_pool(name="work", bufs=3))
        wide = stack.enter_context(tc.tile_pool(name="wide", bufs=5))
        small = stack.enter_context(tc.tile_pool(name="small", bufs=4))
        psum_t = stack.enter_context(tc.psum_pool(name="psum_t", bufs=2))
        psum_acc = stack.enter_context(tc.psum_pool(name="psum_acc", bufs=4))
        psum_z = stack.enter_context(tc.psum_pool(name="psum_z", bufs=2))

        x_sb = []
        for g in range(GROUPS):
            x_sb.append(x_pool.tile([P, TILES, D], BF16, name="x_sb", tag="x_sb"))
        w1_sb = const.tile([P, PACK, D], BF16)
        w2_sb = const.tile([P, PACK, D], BF16)
        bias_rows = const.tile([P, 2, D], BF16)
        param_rows = const.tile([P, P], BF16)
        nc.vector.memset(bias_rows[:], 0.0)
        nc.vector.memset(param_rows[:], 0.0)
        nc.sync.dma_start(out=w1_sb[:], in_=w1.rearrange("(ob p) k -> p ob k", p=P))
        nc.sync.dma_start(out=x_sb[0][:], in_=x_groups[0])
        nc.sync.dma_start(out=bias_rows[0:1, 0, :], in_=b1.rearrange("(o f) -> o f", o=1))
        nc.sync.dma_start(out=x_sb[1][:], in_=x_groups[1])
        nc.sync.dma_start(out=x_sb[2][:], in_=x_groups[2])
        nc.sync.dma_start(out=w2_sb[:], in_=w2.rearrange("(ob p) k -> p ob k", p=P))
        nc.sync.dma_start(out=bias_rows[0:1, 1, :], in_=b2.rearrange("(o f) -> o f", o=1))
        nc.sync.dma_start(out=param_rows[0:PACK, :], in_=gamma.rearrange("(t p) -> t p", p=P))
        nc.sync.dma_start(out=param_rows[PACK : 2 * PACK, :], in_=beta.rearrange("(t p) -> t p", p=P))
        for g in range(3, GROUPS):
            nc.sync.dma_start(out=x_sb[g][:], in_=x_groups[g])

        ident_f32 = const.tile([P, P], F32)
        make_identity(nc, ident_f32[:])
        ident_bf = const.tile([P, P], BF16)
        make_identity(nc, ident_bf[:])
        ones = const.tile([P, P], BF16)
        nc.vector.memset(ones[:], 1.0)
        warm = const.tile([P, 1], F32)
        nc.vector.memset(warm[:], 1.0)
        nc.scalar.sqrt(out=warm[:], in_=warm[:])

        def word_transposes(rows, grouped, on_vector):
            words = rows.bitcast(F32)
            planes_ps = psum_t.tile([P, 2, 2 * P], F32, name="planes_ps", tag="tp")
            for b in range(2):
                for u in range(2):
                    nc.tensor.transpose(
                        planes_ps[:, u, b * P : (b + 1) * P], words[:, b, u * P : (u + 1) * P], ident_f32[:]
                    )
            if on_vector:
                nc.vector.tensor_copy(out=grouped.bitcast(F32), in_=planes_ps[:].rearrange("p u c -> p c u"))
            else:
                nc.scalar.copy(out=grouped.bitcast(F32), in_=planes_ps[:].rearrange("p u c -> p c u"))

        def quantise(grouped, codes, scales):
            nc.vector.quantize_mx(
                out=codes.bitcast(FP8X4),
                scales=scales,
                in_=grouped.rearrange("p c t -> p (c t)"),
            )

        w1_grouped = const.tile([P, D, PACK], BF16, align_bytes=64)
        w1_codes = const.tile([P, D], U32, align_bytes=64)
        w1_scales = const.tile([P, D], U8, align_bytes=64)
        word_transposes(w1_sb[:, 0:2, :], w1_grouped[:, 0 : 2 * P, :], True)
        word_transposes(w1_sb[:, 2:4, :], w1_grouped[:, 2 * P : 4 * P, :], False)
        quantise(w1_grouped[:], w1_codes[:], w1_scales[:])

        bias_bc = const.tile([P, 2, D], F32)
        params = const.tile([P, 2 * PACK], F32)
        w2_grouped = const.tile([P, D, PACK], BF16, align_bytes=64)
        w2_codes = const.tile([P, D], U32, align_bytes=64)
        w2_scales = const.tile([P, D], U8, align_bytes=64)

        def spread_bias(i):
            bias_ps = psum_acc.tile([P, D], F32, name="bias_ps", tag="acc")
            nc.tensor.matmul(bias_ps[:], lhsT=ones[:], rhs=bias_rows[:, i, :], start=True, stop=True)
            nc.vector.tensor_copy(out=bias_bc[:, i, :], in_=bias_ps[:])

        def w2_to_partitions():
            param_ps = psum_t.tile([P, P], BF16, name="param_ps", tag="tp")
            nc.tensor.transpose(param_ps[:], param_rows[:], ident_bf[:])
            nc.scalar.copy(out=params[:], in_=param_ps[:, 0 : 2 * PACK])
            for h in range(2):
                w2_ps = psum_t.tile([P, PACK, 2 * P], BF16, name="w2_ps", tag="tp")
                for b in range(2):
                    for t in range(PACK):
                        nc.tensor.transpose(
                            w2_ps[:, t, b * P : (b + 1) * P],
                            w2_sb[:, 2 * h + b, t * P : (t + 1) * P],
                            ident_bf[:],
                        )
                nc.scalar.copy(
                    out=w2_grouped[:, 2 * h * P : 2 * (h + 1) * P, :],
                    in_=w2_ps[:].rearrange("p t c -> p c t"),
                )

        x_grouped, x_codes, x_scales = {}, {}, {}
        llm, sums, neg_mean, std, z = {}, {}, {}, {}, {}
        planes, n_grouped, n_codes, n_scales = {}, {}, {}, {}

        def x_to_partitions(g):
            x_grouped[g] = work.tile([P, GROUP, PACK], BF16, name="x_grouped", align_bytes=64)
            word_transposes(x_sb[g][:], x_grouped[g][:], False)

        def quantise_x(g):
            x_codes[g] = work.tile([P, GROUP], U32, name="x_codes", align_bytes=64)
            x_scales[g] = work.tile([P, GROUP], U8, name="x_scales", align_bytes=64)
            quantise(x_grouped[g][:], x_codes[g][:], x_scales[g][:])

        def first_matmul(g):
            llm[g] = wide.tile([P, TILES, D], F32, name="llm")
            sums[g] = small.tile([P, TILES], F32, name="sums")
            for j in range(TILES):
                cols = slice(j * P, (j + 1) * P)
                acc = psum_acc.tile([P, D], F32, name="acc", tag="acc")
                nc.tensor.matmul_mx(
                    out=acc[:],
                    lhsT=x_codes[g][:, cols].bitcast(FP8X4),
                    lhsT_scale=x_scales[g][:, cols],
                    rhs=w1_codes[:].bitcast(FP8X4),
                    rhs_scale=w1_scales[:],
                    start=True,
                    stop=True,
                )
                nc.vector.scalar_tensor_tensor(
                    out=llm[g][:, j, :],
                    in0=acc[:],
                    scalar=1.0,
                    in1=bias_bc[:, 0, :],
                    op0=ALU.mult,
                    op1=ALU.add,
                    accum_out=sums[g][:, j : j + 1],
                )
            nc.sync.dma_start(out=llm_groups[g], in_=llm[g][:])

        def statistics(g):
            neg_mean[g] = small.tile([P, TILES], F32, name="neg_mean")
            nc.scalar.mul(out=neg_mean[g][:], in_=sums[g][:], mul=-1.0 / D)
            squares = work.tile([P, TILES, D], BF16)
            sum_sq = small.tile([P, TILES], F32)
            for j in range(TILES):
                nc.scalar.activation(
                    out=squares[:, j, :],
                    in_=llm[g][:, j, :],
                    func=ACT.Square,
                    bias=neg_mean[g][:, j : j + 1],
                    scale=1.0,
                    accum_out=sum_sq[:, j : j + 1],
                )
            std[g] = small.tile([P, TILES], F32, name="std")
            nc.scalar.activation(out=std[g][:], in_=sum_sq[:], func=ACT.Sqrt, bias=EPS, scale=1.0 / D)

        def normalise(g):
            rstd = small.tile([P, TILES], F32)
            nc.vector.reciprocal(out=rstd[:], in_=std[g][:])
            z[g] = work.tile([P, TILES, D], F32, name="z")
            for j in range(TILES):
                nc.gpsimd.tensor_scalar(
                    out=z[g][:, j, :],
                    in0=llm[g][:, j, :],
                    scalar1=neg_mean[g][:, j : j + 1],
                    scalar2=rstd[:, j : j + 1],
                    op0=ALU.add,
                    op1=ALU.mult,
                )

        def features_to_partitions(g):
            planes[g] = work.tile([P, PACK, GROUP], BF16, name="planes")
            for h in range(2):
                z_ps = psum_z.tile([P, 2, GROUP], F32, name="z_ps", tag="z_ps")
                for i in range(2):
                    t = 2 * h + i
                    for j in range(TILES):
                        nc.tensor.transpose(
                            z_ps[:, i, j * P : (j + 1) * P], z[g][:, j, t * P : (t + 1) * P], ident_f32[:]
                        )
                for i in range(2):
                    t = 2 * h + i
                    nc.scalar.activation(
                        out=planes[g][:, t, :],
                        in_=z_ps[:, i, :],
                        func=ACT.Identity,
                        bias=params[:, PACK + t : PACK + t + 1],
                        scale=params[:, t : t + 1],
                    )

        def regroup_n(g):
            n_grouped[g] = work.tile([P, GROUP, PACK], BF16, name="n_grouped", align_bytes=64)
            nc.vector.tensor_copy(
                out=n_grouped[g][:].rearrange("p (c i) t -> p c t i", i=4),
                in_=planes[g][:].rearrange("p t (c i) -> p c t i", i=4),
            )

        def quantise_n(g):
            n_codes[g] = work.tile([P, GROUP], U32, name="n_codes", align_bytes=64)
            n_scales[g] = work.tile([P, GROUP], U8, name="n_scales", align_bytes=64)
            quantise(n_grouped[g][:], n_codes[g][:], n_scales[g][:])

        def second_matmul(g):
            q = wide.tile([P, TILES, D], F32)
            for j in range(TILES):
                cols = slice(j * P, (j + 1) * P)
                acc = psum_acc.tile([P, D], F32, name="acc", tag="acc")
                nc.tensor.matmul_mx(
                    out=acc[:],
                    lhsT=n_codes[g][:, cols].bitcast(FP8X4),
                    lhsT_scale=n_scales[g][:, cols],
                    rhs=w2_codes[:].bitcast(FP8X4),
                    rhs_scale=w2_scales[:],
                    start=True,
                    stop=True,
                )
                nc.vector.tensor_add(out=q[:, j, :], in0=acc[:], in1=bias_bc[:, 1, :])
                nc.sync.dma_start(out=q_groups[g][:, j, :], in_=q[:, j, :])

        def run(stage, g):
            if 0 <= g < GROUPS:
                stage(g)

        for step in range(GROUPS + LAST_LAG):
            run(x_to_partitions, step)
            run(regroup_n, step - 6)
            run(quantise_x, step - 1)
            run(quantise_n, step - 6)
            run(normalise, step - 4)
            run(first_matmul, step - 2)
            run(second_matmul, step - 7)
            run(statistics, step - 3)
            run(features_to_partitions, step - 5)
            if step == 0:
                spread_bias(0)
            if step == W2_TRANSPOSE_STEP:
                w2_to_partitions()
            if step == W2_QUANTISE_STEP:
                quantise(w2_grouped[:], w2_codes[:], w2_scales[:])
                spread_bias(1)
